import numpy as np
import ml_dtypes


def mxq(x, axis, fmt="e4m3"):
    dtype, down = {"e4m3": (ml_dtypes.float8_e4m3fn, 7), "e5m2": (ml_dtypes.float8_e5m2, 14)}[fmt]
    v = np.moveaxis(np.asarray(x, np.float32).astype(ml_dtypes.bfloat16).astype(np.float64), axis, -1)
    blocks = v.reshape(v.shape[:-1] + (-1, 32))
    amax = np.abs(blocks).max(-1, keepdims=True)
    byte = np.maximum(np.where(amax > 0, np.frexp(amax)[1] - 1 + 127, 0) - down, 1)
    scale = np.exp2(byte - 127.0)
    codes = (blocks / scale).astype(np.float32).astype(dtype).astype(np.float64)
    return np.moveaxis((codes * scale).reshape(v.shape), -1, axis)


WIDE = False


def mx_kscale(k):
    if not WIDE:
        return np.ones(k)
    levels = np.array([10, -10, 5, -5, 0])
    if k % 512:
        return np.exp2(np.random.permutation(np.resize(levels, k // 32))).repeat(32)
    a = np.empty((k // 512, 16))
    for p in range(k // 512):
        a[p, :8] = np.random.permutation(np.resize(levels, 8))
        for g in range(8):
            far = levels[np.abs(levels - a[p, g]) >= 10]
            a[p, g + 8] = far[np.random.randint(len(far))]
    return np.exp2(a.ravel()).repeat(32)


BF16 = ml_dtypes.bfloat16


def bf(x):
    return np.asarray(x, np.float32).astype(BF16)


def f64(x):
    return np.asarray(x).astype(np.float64)


B, C, H, W = 128, 1024, 3, 3
C3, CH, P = 3 * C, C // 2, H * W


def sigmoid(v):
    return 1.0 / (1.0 + np.exp(-v))


def draw0():
    s, t = mx_kscale(C3), mx_kscale(CH)
    n = np.random.standard_normal
    return {
        "fv": bf(n((B, C3, H, W)) * s[None, :, None, None]),
        "ft": bf(n((B, C))),
        "Wa": bf(n((CH, C3)) / np.sqrt(C3) / s[None, :] * t[:, None]),
        "ba": bf(n(CH) * 0.3 * t),
        "Wb": bf(n((C, CH)) * 2.0 / np.sqrt(CH) / t[None, :]),
        "bb": bf(n(C) * 0.5),
        "Wfc2": bf(n((C, C)) / np.sqrt(C)),
        "bfc2": bf(n(C) * 0.3),
    }


def core(fv, ft, Wa, ba, Wb, bb, Wfc2, bfc2):
    h = np.maximum((mxq(f64(Wa), 1, "e4m3") @ mxq(f64(fv).reshape(B, C3, P), 1, "e4m3")) + f64(ba)[None, :, None], 0.0)
    fv2 = (mxq(f64(Wb), 1, "e4m3") @ mxq(h, 1, "e4m3")) + f64(bb)[None, :, None]
    gate = sigmoid(fv2.mean(axis=2))
    ft2 = f64(ft) @ f64(Wfc2).T + f64(bfc2)
    return ft2 + ft2 * gate


def e4m3fn_bytes(y):
    return np.clip(np.asarray(y, np.float64), -448.0, 448.0).astype(np.float32).astype(ml_dtypes.float8_e4m3fn).view(np.uint8)


def e4m3fn_values(b):
    return np.asarray(b, np.uint8).view(ml_dtypes.float8_e4m3fn).astype(np.float64)


def setup_inputs():
    d = draw0()
    x0 = np.asarray(d['fv']).astype(np.float64)
    s = (np.max(np.abs(x0), axis=(0, 2, 3), keepdims=True) / 448.0).astype(np.float32)
    out = {}
    for k, v in d.items():
        if k == 'fv':
            out['fv_bytes'] = e4m3fn_bytes(x0 / s.astype(np.float64))
            out['fv_scale'] = s
        else:
            out[k] = v
    return out


def reference(fv_bytes, fv_scale, ft, Wa, ba, Wb, bb, Wfc2, bfc2):
    return core(e4m3fn_values(fv_bytes) * fv_scale.astype(np.float64), ft, Wa, ba, Wb, bb, Wfc2, bfc2)

@@ -1,0 +1,378 @@
+from contextlib import ExitStack
+
+import concourse.mybir as mybir
+from concourse.masks import make_identity
+
+F32 = mybir.dt.float32
+BF16 = mybir.dt.bfloat16
+U32 = mybir.dt.uint32
+U8 = mybir.dt.uint8
+FP8 = mybir.dt.float8_e4m3fn
+FP8X4 = mybir.dt.float8_e4m3fn_x4
+ALU = mybir.AluOpType
+ACT = mybir.ActivationFunctionType
+
+B, C3, HID, C = 128, 3072, 512, 1024
+PIX = 9
+P = 128
+G = C3 // 512
+
+FLOPS = 2 * (C3 * HID + HID * C) * B * PIX + 2 * B * C * C
+
+
+def tile_joint_module_pb_kernel(tc, fv_bytes, fv_scale, ft, Wa, ba, Wb, bb, Wfc2, bfc2, out):
+    nc = tc.nc
+    with ExitStack() as ctx:
+        keep = ctx.enter_context(tc.tile_pool(name="keep", bufs=1))
+        raw = ctx.enter_context(tc.tile_pool(name="raw", bufs=4))
+        work = ctx.enter_context(tc.tile_pool(name="work", bufs=2))
+        psum = ctx.enter_context(tc.psum_pool(name="psum", bufs=1))
+
+        id_f32 = keep.tile([P, P], F32, name="id_f32")
+        id_bf = keep.tile([P, P], BF16, name="id_bf")
+        make_identity(nc, id_bf[:])
+        make_identity(nc, id_f32[:])
+
+        sc = keep.tile([P, G, 4], F32, name="sc")
+        ba_t = keep.tile([P, 4], BF16, name="ba_t")
+        bb_t = keep.tile([P, C], BF16, name="bb_t")
+        bf_t = keep.tile([P, C], BF16, name="bf_t")
+        dummy = keep.tile([P, 1], F32, name="dummy")
+
+
+        fv_rows = fv_bytes.rearrange("b c i j -> b (c i j)")
+        wa_rows = Wa.rearrange("(m t) k -> m t k", t=4)
+        wb_rows = Wb.rearrange("(i p) m -> p i m", p=P)
+        w2_rows = Wfc2.rearrange("(i p) k -> p i k", p=P)
+
+        fvb = {}
+
+        def load_fv(g):
+            for h in range(2):
+                tb = raw.tile([P, 2304], U8, name="fvb", tag="fvb", bufs=6)
+                c0 = g * 4608 + h * 2304
+                nc.sync.dma_start(out=tb[:], in_=fv_rows[:, c0 : c0 + 2304])
+                fvb[g, h] = tb
+
+        wa_raw = {}
+
+        def load_wa(g):
+            t = raw.tile([P, 4, 512], BF16, name="wa_raw", tag="wa_raw", bufs=3)
+            nc.sync.dma_start(out=t[:], in_=wa_rows[:, :, 512 * g : 512 * (g + 1)])
+            wa_raw[g] = t
+
+        w2_raw = {}
+
+        def load_w2(h):
+            t = raw.tile([P, 4, 1024], BF16, name="w2_raw", tag="big8", bufs=2)
+            nc.sync.dma_start(out=t[:], in_=w2_rows[:, 4 * h : 4 * h + 4, :])
+            w2_raw[h] = t
+
+        ft_raw = keep.tile([P, C], BF16, name="ft_raw")
+        wb_raw = raw.tile([P, 8, HID], BF16, name="wb_raw", tag="wb_raw", bufs=1)
+
+        nc.scalar.dma_start(out=sc[:], in_=fv_scale.rearrange("o (g p t) i j -> p (o g) (t i j)", p=P, t=4))
+        nc.scalar.dma_start(out=ba_t[:], in_=ba.rearrange("(p t) -> p t", t=4))
+        load_fv(0)
+        load_wa(0)
+        load_fv(1)
+        load_wa(1)
+        load_fv(2)
+        load_wa(2)
+        nc.vector.memset(dummy[:], 0.0)
+        nc.scalar.activation(out=dummy[:], in_=dummy[:], func=ACT.Sigmoid)
+
+        wide = {}
+
+        def widen(g, plan):
+            t = work.tile([P, 4608], BF16, name="wide", tag="wide", bufs=5)
+            wide[g] = t
+            for q, e in enumerate(plan):
+                src = fvb[g, q // 2][:, (q % 2) * 1152 : (q % 2 + 1) * 1152].bitcast(FP8)
+                dst = t[:, q * 1152 : (q + 1) * 1152]
+                if e == "S":
+                    nc.scalar.copy(out=dst, in_=src)
+                else:
+                    nc.vector.tensor_copy(out=dst, in_=src)
+
+        turn = {"n": 0, "banks": 3}
+
+        def x_bank(dtype, shape, name):
+            k = turn["n"] % turn["banks"]
+            turn["n"] += 1
+            return psum.tile(shape, dtype, name=name, tag="x%d" % k)
+
+        def s_bank(dtype, shape, name):
+            return psum.tile(shape, dtype, name=name, tag="x3")
+
+        def transposes_fv(bank, slot, g, pix):
+            for t in range(4):
+                e = 9 * t + pix
+                nc.tensor.transpose(bank[:, slot, t, :], wide[g][:, e : e + 36 * 127 + 1 : 36], id_bf[:])
+
+        def scaled(dst, bank, slots, scale):
+            nc.vector.tensor_tensor(
+                out=dst, in0=bank[:, slots, :, :].rearrange("p x t b -> p x b t"), in1=scale, op=ALU.mult
+            )
+
+        codes, planes = {}, {}
+
+        def quantize(key, src, n):
+            codes[key] = keep.tile([P, n], U32, name="codes_" + key, align_bytes=64)
+            planes[key] = keep.tile([P, n], U8, name="planes_" + key, align_bytes=64)
+            nc.vector.quantize_mx(out=codes[key][:].bitcast(FP8X4), scales=planes[key][:], in_=src)
+
+        grouped = {}
+
+        def prep_fv(kind, g, pixels):
+            t = work.tile([P, 4, P, 4], BF16, name="fv_grouped", tag="fv_grouped", bufs=4, align_bytes=64)
+            for h in range(2):
+                bank = x_bank(BF16, [P, 2, 4, P], "fv_t")
+                for s in range(2):
+                    transposes_fv(bank, s, g, pixels[2 * h + s])
+                scale = sc[:, g, :].unsqueeze(1).unsqueeze(1).to_broadcast([P, 2, P, 4])
+                scaled(t[:, 2 * h : 2 * h + 2, :, :], bank, slice(0, 2), scale)
+            grouped[kind + str(g)] = t
+
+        def quant_fv(kind, g):
+            quantize(kind + str(g), grouped[kind + str(g)][:].rearrange("p x b t -> p (x b t)"), 512)
+
+        def prep_c(g):
+            t = work.tile([P, 2, P, 4], BF16, name="c_grouped", tag="c_grouped", bufs=2, align_bytes=64)
+            bank = x_bank(BF16, [P, 2, 4, P], "fv_t")
+            for s in range(2):
+                transposes_fv(bank, s, g + s, 8)
+            scale = sc[:, g : g + 2, :].unsqueeze(2).to_broadcast([P, 2, P, 4])
+            scaled(t[:], bank, slice(0, 2), scale)
+            grouped["C" + str(g)] = t
+
+        def quant_c(g):
+            quantize("C" + str(g), grouped["C" + str(g)][:].rearrange("p x b t -> p (x b t)"), 256)
+
+        wa_grouped = {}
+
+        def prep_wa(g):
+            t = work.tile([P, 2048], BF16, name="wa_grouped", tag="wa_grouped", bufs=2, align_bytes=64)
+            words = wa_raw[g][:].rearrange("p t k -> p (t k)").bitcast(F32)
+            for h in range(2):
+                bank = s_bank(F32, [P, 2, 2, P], "wa_t")
+                for s in range(2):
+                    for u in range(2):
+                        w0 = 256 * (2 * h + s) + u
+                        nc.tensor.transpose(bank[:, s, u, :], words[:, w0 : w0 + 255 : 2], id_f32[:])
+                dst = t[:, 1024 * h : 1024 * (h + 1)].bitcast(F32).rearrange("p (s j u) -> p s j u", s=2, u=2)
+                nc.scalar.copy(out=dst, in_=bank[:].rearrange("p s u j -> p s j u"))
+            wa_grouped[g] = t
+
+        def quant_wa(g):
+            quantize("W" + str(g), wa_grouped[g][:], 512)
+
+        wb_grouped = keep.tile([P, 4096], BF16, name="wb_grouped", align_bytes=64)
+
+        def prep_wb(h):
+            words = wb_raw[:].rearrange("p i m -> p (i m)").bitcast(F32)
+            bank = s_bank(F32, [P, 2, 2, P], "wb_t")
+            for s in range(2):
+                for u in range(2):
+                    w0 = 256 * (2 * h + s) + u
+                    nc.tensor.transpose(bank[:, s, u, :], words[:, w0 : w0 + 255 : 2], id_f32[:])
+            dst = wb_grouped[:, 1024 * h : 1024 * (h + 1)].bitcast(F32).rearrange("p (s j u) -> p s j u", s=2, u=2)
+            nc.scalar.copy(out=dst, in_=bank[:].rearrange("p s u j -> p s j u"))
+
+        ft_t = keep.tile([P, 4, P], F32, name="ft_t")
+
+        def prep_ft():
+            bank = s_bank(F32, [P, 4, P], "ft_tp")
+            for w in range(4):
+                nc.tensor.transpose(bank[:, w, :], ft_raw[:].bitcast(F32)[:, 128 * w : 128 * (w + 1)], id_f32[:])
+            nc.scalar.copy(out=ft_t[:], in_=bank[:])
+
+        w2_t = {}
+
+        def prep_w2(h, w):
+            if w == 0:
+                w2_t[h] = work.tile([P, 4, 512], F32, name="w2_t", tag="w2_t", bufs=1)
+            words = w2_raw[h][:].rearrange("p i k -> p (i k)").bitcast(F32)
+            bank = s_bank(F32, [P, 4, P], "w2_tp")
+            for i in range(4):
+                nc.tensor.transpose(bank[:, i, :], words[:, 512 * i + 128 * w : 512 * i + 128 * (w + 1)], id_f32[:])
+            nc.scalar.copy(out=w2_t[h][:, w, :], in_=bank[:].rearrange("p i o -> p (i o)"))
+
+        ft2 = keep.tile([P, C], F32, name="ft2")
+
+        def fc2(h):
+            bank = s_bank(F32, [P, 512], "fc2_acc")
+            for w in range(4):
+                for e in range(2):
+                    nc.tensor.matmul(
+                        bank[:],
+                        lhsT=ft_t[:, w, :].bitcast(BF16)[:, e : e + 255 : 2],
+                        rhs=w2_t[h][:, w, :].bitcast(BF16)[:, e : e + 1023 : 2],
+                        start=(w == 0 and e == 0),
+                        stop=(w == 3 and e == 1),
+                    )
+            cols = slice(512 * h, 512 * (h + 1))
+            nc.vector.tensor_tensor(out=ft2[:, cols], in0=bank[:], in1=bf_t[:, cols], op=ALU.add)
+
+        acc = {}
+
+        def conv1(kind, g):
+            for t in range(4):
+                if g == 0:
+                    acc[t] = psum.tile([P, 512], F32, name="acc", tag="acc%d" % t)
+                nc.tensor.matmul_mx(
+                    out=acc[t][:],
+                    lhsT=codes["W" + str(g)][:, P * t : P * (t + 1)].bitcast(FP8X4),
+                    lhsT_scale=planes["W" + str(g)][:, P * t : P * (t + 1)],
+                    rhs=codes[kind + str(g)][:].bitcast(FP8X4),
+                    rhs_scale=planes[kind + str(g)][:],
+                    start=(g == 0),
+                    stop=(g == G - 1),
+                )
+
+        hid = {}
+
+        def relu(kind):
+            t4 = work.tile([P, 4, 512], BF16, name="hid", tag="hid", bufs=1)
+            for t in range(4):
+                nc.scalar.activation(out=t4[:, t, :], in_=acc[t][:], func=ACT.Relu, bias=ba_t[:, t : t + 1])
+            hid[kind] = t4
+
+        def interleave(kind, n):
+            t = work.tile([P, n, 4], BF16, name="hid_grouped" + kind, tag="hid_grouped_%d" % n, bufs=1, align_bytes=64)
+            nc.vector.tensor_copy(
+                out=t[:].rearrange("p (c i) t -> p c t i", i=4),
+                in_=hid[kind][:, :, 0:n].rearrange("p t (c i) -> p c t i", i=4),
+            )
+            grouped["H" + kind] = t
+
+        def quant_h(kind, n):
+            quantize("H" + kind, grouped["H" + kind][:].rearrange("p n t -> p (n t)"), n)
+
+        s2 = {}
+
+        def conv2(kind, npix, first, last):
+            for x in range(npix):
+                for h in range(2):
+                    nc.tensor.matmul_mx(
+                        out=s2[h][:],
+                        lhsT=codes["H" + kind][:, P * x : P * (x + 1)].bitcast(FP8X4),
+                        lhsT_scale=planes["H" + kind][:, P * x : P * (x + 1)],
+                        rhs=codes["WB"][:, 512 * h : 512 * (h + 1)].bitcast(FP8X4),
+                        rhs_scale=planes["WB"][:, 512 * h : 512 * (h + 1)],
+                        start=(first and x == 0),
+                        stop=(last and x == npix - 1),
+                    )
+
+        A, Bq = [0, 1, 2, 3], [4, 5, 6, 7]
+        plans = {0: "SVVV", 1: "SSVV", 2: "SSSV", 3: "SSSS", 4: "SSSS", 5: "SSSS"}
+        widen(0, plans[0])
+        for s in range(8):
+            if s == 0:
+                load_fv(3)
+                load_wa(3)
+                nc.sync.dma_start(out=ft_raw[:], in_=ft)
+                load_w2(0)
+            if s == 1:
+                load_fv(4)
+                load_wa(4)
+                nc.sync.dma_start(out=wb_raw[:], in_=wb_rows)
+            if s == 2:
+                load_fv(5)
+                load_wa(5)
+                load_w2(1)
+                nc.sync.dma_start(out=bf_t[:], in_=bfc2.partition_broadcast(P))
+                nc.sync.dma_start(out=bb_t[:], in_=bb.partition_broadcast(P))
+            if s + 1 < G:
+                widen(s + 1, plans[s + 1])
+            if s < G:
+                prep_fv("A", s, A)
+                prep_wa(s)
+            if 1 <= s <= G:
+                conv1("A", s - 1)
+            if s == G:
+                relu("A")
+            if 2 <= s:
+                prep_fv("B", s - 2, Bq)
+                if s % 2 == 1:
+                    prep_c(s - 3)
+            if s == 2:
+                prep_ft()
+                prep_w2(0, 0)
+                prep_w2(0, 1)
+            if s == 3:
+                prep_w2(0, 2)
+                prep_w2(0, 3)
+                prep_wb(0)
+                prep_wb(1)
+            if s == 4:
+                fc2(0)
+                prep_wb(2)
+                prep_wb(3)
+            if s == 5:
+                prep_w2(1, 0)
+                prep_w2(1, 1)
+            if s == 6:
+                prep_w2(1, 2)
+                prep_w2(1, 3)
+                fc2(1)
+            if s < G:
+                quant_fv("A", s)
+                quant_wa(s)
+            if 2 <= s:
+                quant_fv("B", s - 2)
+                if s % 2 == 1:
+                    quant_c(s - 3)
+            if s == 5:
+                quantize("WB", wb_grouped[:], 1024)
+            if s == 6:
+                interleave("A", 512)
+                quant_h("A", 512)
+                conv1("B", 0)
+                conv1("B", 1)
+                conv1("B", 2)
+            if s == 7:
+                conv1("B", 3)
+                turn["banks"] = 2
+                s2[0] = psum.tile([P, 512], F32, name="s2_0", tag="x3")
+                s2[1] = psum.tile([P, 512], F32, name="s2_1", tag="x2")
+                conv2("A", 4, True, False)
+        conv1("B", 4)
+        conv1("B", 5)
+        relu("B")
+        cbank = x_bank(F32, [P, 4, P], "acc_c")
+        for t in range(4):
+            for g in range(G):
+                key = "C" + str(g - g % 2)
+                nc.tensor.matmul_mx(
+                    out=cbank[:, t, :],
+                    lhsT=codes["W" + str(g)][:, P * t : P * (t + 1)].bitcast(FP8X4),
+                    lhsT_scale=planes["W" + str(g)][:, P * t : P * (t + 1)],
+                    rhs=codes[key][:, P * (g % 2) : P * (g % 2 + 1)].bitcast(FP8X4),
+                    rhs_scale=planes[key][:, P * (g % 2) : P * (g % 2 + 1)],
+                    start=(g == 0),
+                    stop=(g == G - 1),
+                )
+        hid["C"] = work.tile([P, 4, P], BF16, name="hid_c", tag="hid_c", bufs=1)
+        for t in range(4):
+            nc.scalar.activation(out=hid["C"][:, t, :], in_=cbank[:, t, :], func=ACT.Relu, bias=ba_t[:, t : t + 1])
+        interleave("B", 512)
+        interleave("C", P)
+        quant_h("B", 512)
+        quant_h("C", P)
+        conv2("B", 4, False, False)
+        conv2("C", 1, False, True)
+
+        z = keep.tile([P, C], F32, name="z")
+        gate = keep.tile([P, C], F32, name="gate")
+        res = keep.tile([P, C], F32, name="res")
+        for h in range(2):
+            cols = slice(512 * h, 512 * (h + 1))
+            nc.vector.scalar_tensor_tensor(
+                out=z[:, cols], in0=s2[h][:], scalar=1.0 / PIX, in1=bb_t[:, cols], op0=ALU.mult, op1=ALU.add
+            )
+            nc.scalar.activation(out=gate[:, cols], in_=z[:, cols], func=ACT.Sigmoid)
+            nc.vector.scalar_tensor_tensor(
+                out=res[:, cols], in0=gate[:, cols], scalar=1.0, in1=ft2[:, cols], op0=ALU.add, op1=ALU.mult
+            )
+            nc.sync.dma_start(out=out[:, cols], in_=res[:, cols])

@@ -17,7 +17,42 @@ PIX = 9
 P = 128
 G = C3 // 512
 
+WARM = 56
+
 FLOPS = 2 * (C3 * HID + HID * C) * B * PIX + 2 * B * C * C
+
+
+LOADS = "f0.0 f0.1 k0 f1.0 f1.1 k1 f2.0 f2.1 20 f3.0 f3.1 k2 21 f4.0 f4.1 k3 f5.0 i f5.1 t i2 k4 k5 b"
+STEPS = [
+    "v0.0 w0.1 v0.2 w0.3 Tk0.0 v1.0 w1.1 TA0.0 v1.2 TA0.1 Ek0.0 EA0.0",
+    "w1.3 Tk0.1 v2.0 Ek0.1 v2.1 TA1.0 w2.2 Tk1.0 qW0 TA1.1 EA0.1",
+    "Ek1.0 EA1.0",
+    "w2.3 T20.0 qA0 E20.0 TA2.0 EA1.1",
+    "w3.0 Tk1.1 mm.A.0.0 EA2.0",
+    "mm.A.0.1 Ek1.1 mm.A.0.2 w3.1 mm.A.0.3 qA1 T20.1 qW1 TA2.1 E20.1 TB0.0 EA2.1",
+    "w3.2 T20.2 mm.A.1.0 mm.A.1.1 EB0.0",
+    "mm.A.1.2 E20.2 mm.A.1.3 TB0.1 w3.3 qA2 Tk2.0 EB0.1",
+    "TB1.0 Ek2.0 TB1.1 w4.0 EB1.0",
+    "T20.3 TA3.0 qB0 E20.3 TA3.1 v4.1 w4.2 EB1.1",
+    "Tf w4.3 v5.0 qB1 Ef TA4.0 EA3.0",
+    "w5.1 mF.0.0 EA3.1",
+    "mF.0.1 w5.2 mF.0.2 EA4.0",
+    "mF.0.3 mF.0.4 w5.3 mF.0.5 mF.0.6 qA3 mF.0.7 TA4.1 EF0 TA5.0 EA4.1",
+    "Tk2.1 TA5.1 Ek2.1 EA5.0",
+    "TB2.0 Tk3.0 qA4 TB2.1 Ek3.0 qW2 EA5.1",
+    "Tk3.1 mm.A.2.0 Ek3.1 EB2.0",
+    "mm.A.2.1 mm.A.2.2 qA5 mm.A.2.3 qW3 Tk4.0 EB2.1",
+    "TB3.0 Ek4.0 mm.A.3.0 mm.A.3.1 EB3.0",
+    "mm.A.3.2 mm.A.3.3 Tk4.1 qB2 TB3.1 Ek4.1 TB4.0 EB3.1",
+    "Tk5.0 TB4.1 Ek5.0 qW4 TC0.0 qB3 Tk5.1 EB4.0",
+    "mm.A.4.0 Ek5.1 mm.A.4.1 qW5 mm.A.4.2 EB4.1",
+    "mm.A.4.3 mm.A.5.0 mm.A.5.1 RA0 EC0.0",
+    "Tb3 RA1 mm.A.5.2 mm.A.5.3 Eb3 qB4 mm.B.0.0 mm.B.0.1 RA2 qC0 T21.0 TB5.0 RA3 E21.0 mm.B.0.2 IA mm.B.0.3 mm.B.1.0 T21.1 mm.B.1.1 EB5.0",
+    "E21.1 mm.B.1.2 mm.B.1.3 Tb2 qhA mm.B.2.0 Eb2 mm.B.2.1 mm.B.2.2 Tb0 mm.B.2.3 Eb0 mm.B.3.0 mm.B.3.1 Tb1 mm.B.3.2 Eb1 mm.B.3.3 mm.B.4.0 qb T21.2 mm.B.4.1 E21.2 mm.B.4.2 mm.B.4.3 T21.3 TB5.1 E21.3 TC2.0 EB5.1",
+    "mF.1.0 mF.1.1 mF.1.2 EC2.0",
+    "mF.1.3 mF.1.4 mF.1.5 mF.1.6 mF.1.7 qB5 TC4.0 qC2 mm.B.5.0 EF1 mm.B.5.1 RB0 mm.B.5.2 EC4.0",
+    "mm.B.5.3 RB1 ms.A.0.0 ms.A.0.1 ms.A.1.0 RB2 ms.A.1.1 qC4 ms.A.2.0 RB3 mm.C.0.4 IB mm.C.1.4 mm.C.2.4 mm.C.3.4 mm.C.4.4 mm.C.5.4 qhB ms.A.2.1 RC0 ms.A.3.0 RC1 ms.A.3.1 RC2 ms.B.0.0 RC3 ms.B.0.1 IC ms.B.1.0 ms.B.1.1 qhC ms.B.2.0 ms.B.2.1 ms.B.3.0 ms.B.3.1 ms.C.0.0 ms.C.0.1",
+]
 
 
 def tile_joint_module_pb_kernel(tc, fv_bytes, fv_scale, ft, Wa, ba, Wb, bb, Wfc2, bfc2, out):
@@ -39,6 +74,7 @@ def tile_joint_module_pb_kernel(tc, fv_bytes, fv_scale, ft, Wa, ba, Wb, bb, Wfc2
         bf_t = keep.tile([P, C], BF16, name="bf_t")
         dummy = keep.tile([P, 1], F32, name="dummy")
 
+        ctx.enter_context(tc.manual_schedule())
 
         fv_rows = fv_bytes.rearrange("b c i j -> b (c i j)")
         wa_rows = Wa.rearrange("(m t) k -> m t k", t=4)
@@ -46,13 +82,6 @@ def tile_joint_module_pb_kernel(tc, fv_bytes, fv_scale, ft, Wa, ba, Wb, bb, Wfc2
         w2_rows = Wfc2.rearrange("(i p) k -> p i k", p=P)
 
         fvb = {}
-
-        def load_fv(g):
-            for h in range(2):
-                tb = raw.tile([P, 2304], U8, name="fvb", tag="fvb", bufs=6)
-                c0 = g * 4608 + h * 2304
-                nc.sync.dma_start(out=tb[:], in_=fv_rows[:, c0 : c0 + 2304])
-                fvb[g, h] = tb
 
         wa_raw = {}
 
@@ -69,31 +98,24 @@ def tile_joint_module_pb_kernel(tc, fv_bytes, fv_scale, ft, Wa, ba, Wb, bb, Wfc2
             w2_raw[h] = t
 
         ft_raw = keep.tile([P, C], BF16, name="ft_raw")
-        wb_raw = raw.tile([P, 8, HID], BF16, name="wb_raw", tag="wb_raw", bufs=1)
+        wb_raw = {}
 
         nc.scalar.dma_start(out=sc[:], in_=fv_scale.rearrange("o (g p t) i j -> p (o g) (t i j)", p=P, t=4))
         nc.scalar.dma_start(out=ba_t[:], in_=ba.rearrange("(p t) -> p t", t=4))
-        load_fv(0)
-        load_wa(0)
-        load_fv(1)
-        load_wa(1)
-        load_fv(2)
-        load_wa(2)
         nc.vector.memset(dummy[:], 0.0)
         nc.scalar.activation(out=dummy[:], in_=dummy[:], func=ACT.Sigmoid)
 
         wide = {}
 
-        def widen(g, plan):
-            t = work.tile([P, 4608], BF16, name="wide", tag="wide", bufs=5)
-            wide[g] = t
-            for q, e in enumerate(plan):
-                src = fvb[g, q // 2][:, (q % 2) * 1152 : (q % 2 + 1) * 1152].bitcast(FP8)
-                dst = t[:, q * 1152 : (q + 1) * 1152]
-                if e == "S":
-                    nc.scalar.copy(out=dst, in_=src)
-                else:
-                    nc.vector.tensor_copy(out=dst, in_=src)
+        def widen(g, q, on_vector):
+            if g not in wide:
+                wide[g] = work.tile([P, 4608], BF16, name="wide", tag="wide", bufs=6)
+            src = fvb[g, q // 2][:, (q % 2) * 1152 : (q % 2 + 1) * 1152].bitcast(FP8)
+            dst = wide[g][:, q * 1152 : (q + 1) * 1152]
+            if on_vector:
+                nc.vector.tensor_copy(out=dst, in_=src)
+            else:
+                nc.scalar.copy(out=dst, in_=src)
 
         turn = {"n": 0, "banks": 3}
 
@@ -105,10 +127,17 @@ def tile_joint_module_pb_kernel(tc, fv_bytes, fv_scale, ft, Wa, ba, Wb, bb, Wfc2
         def s_bank(dtype, shape, name):
             return psum.tile(shape, dtype, name=name, tag="x3")
 
+        by_matmul = {"left": WARM}
+
         def transposes_fv(bank, slot, g, pix):
             for t in range(4):
                 e = 9 * t + pix
-                nc.tensor.transpose(bank[:, slot, t, :], wide[g][:, e : e + 36 * 127 + 1 : 36], id_bf[:])
+                src = wide[g][:, e : e + 36 * 127 + 1 : 36]
+                if by_matmul["left"] > 0:
+                    by_matmul["left"] -= 1
+                    nc.tensor.matmul(bank[:, slot, t, :], lhsT=src, rhs=id_bf[:], start=True, stop=True)
+                else:
+                    nc.tensor.transpose(bank[:, slot, t, :], src, id_bf[:])
 
         def scaled(dst, bank, slots, scale):
             nc.vector.tensor_tensor(
@@ -124,119 +153,158 @@ def tile_joint_module_pb_kernel(tc, fv_bytes, fv_scale, ft, Wa, ba, Wb, bb, Wfc2
 
         grouped = {}
 
-        def prep_fv(kind, g, pixels):
-            t = work.tile([P, 4, P, 4], BF16, name="fv_grouped", tag="fv_grouped", bufs=4, align_bytes=64)
-            for h in range(2):
-                bank = x_bank(BF16, [P, 2, 4, P], "fv_t")
-                for s in range(2):
-                    transposes_fv(bank, s, g, pixels[2 * h + s])
-                scale = sc[:, g, :].unsqueeze(1).unsqueeze(1).to_broadcast([P, 2, P, 4])
-                scaled(t[:, 2 * h : 2 * h + 2, :, :], bank, slice(0, 2), scale)
-            grouped[kind + str(g)] = t
+        def fill(kind, g, h):
+            bank = x_bank(BF16, [P, 2, 4, P], "fv_t")
+            for s in range(2):
+                if kind == "C":
+                    transposes_fv(bank, s, g + s, 8)
+                else:
+                    transposes_fv(bank, s, g, (0 if kind == "A" else 4) + 2 * h + s)
+            fbank[kind, g, h] = bank
+
+        fbank = {}
+
+        def empty(kind, g, h):
+            bank = fbank[kind, g, h]
+            if kind == "C":
+                t = work.tile([P, 2, P, 4], BF16, name="c_grouped", tag="c_grouped", bufs=2, align_bytes=64)
+                scaled(t[:], bank, slice(0, 2), sc[:, g : g + 2, :].unsqueeze(2).to_broadcast([P, 2, P, 4]))
+                grouped["C" + str(g)] = t
+                return
+            if h == 0:
+                grouped[kind + str(g)] = work.tile(
+                    [P, 4, P, 4], BF16, name="fv_grouped", tag="fv_grouped", bufs=3, align_bytes=64
+                )
+            t = grouped[kind + str(g)]
+            scale = sc[:, g, :].unsqueeze(1).unsqueeze(1).to_broadcast([P, 2, P, 4])
+            scaled(t[:, 2 * h : 2 * h + 2, :, :], bank, slice(0, 2), scale)
 
         def quant_fv(kind, g):
             quantize(kind + str(g), grouped[kind + str(g)][:].rearrange("p x b t -> p (x b t)"), 512)
-
-        def prep_c(g):
-            t = work.tile([P, 2, P, 4], BF16, name="c_grouped", tag="c_grouped", bufs=2, align_bytes=64)
-            bank = x_bank(BF16, [P, 2, 4, P], "fv_t")
-            for s in range(2):
-                transposes_fv(bank, s, g + s, 8)
-            scale = sc[:, g : g + 2, :].unsqueeze(2).to_broadcast([P, 2, P, 4])
-            scaled(t[:], bank, slice(0, 2), scale)
-            grouped["C" + str(g)] = t
 
         def quant_c(g):
             quantize("C" + str(g), grouped["C" + str(g)][:].rearrange("p x b t -> p (x b t)"), 256)
 
         wa_grouped = {}
 
-        def prep_wa(g):
-            t = work.tile([P, 2048], BF16, name="wa_grouped", tag="wa_grouped", bufs=2, align_bytes=64)
-            words = wa_raw[g][:].rearrange("p t k -> p (t k)").bitcast(F32)
-            for h in range(2):
-                bank = s_bank(F32, [P, 2, 2, P], "wa_t")
-                for s in range(2):
-                    for u in range(2):
-                        w0 = 256 * (2 * h + s) + u
-                        nc.tensor.transpose(bank[:, s, u, :], words[:, w0 : w0 + 255 : 2], id_f32[:])
-                dst = t[:, 1024 * h : 1024 * (h + 1)].bitcast(F32).rearrange("p (s j u) -> p s j u", s=2, u=2)
-                nc.scalar.copy(out=dst, in_=bank[:].rearrange("p s u j -> p s j u"))
-            wa_grouped[g] = t
+        side_bank = {}
+
+        def fill_words(key, words, base):
+            side_bank[key] = s_bank(F32, [P, 2, 2, P], "wt")
+            for s in range(2):
+                for u in range(2):
+                    w0 = base + 256 * s + u
+                    nc.tensor.transpose(side_bank[key][:, s, u, :], words[:, w0 : w0 + 255 : 2], id_f32[:])
+
+        def empty_words(key, dst):
+            nc.scalar.copy(
+                out=dst.bitcast(F32).rearrange("p (s j u) -> p s j u", s=2, u=2),
+                in_=side_bank[key][:].rearrange("p s u j -> p s j u"),
+            )
+
+        def fill_wa(g, h):
+            fill_words(("k", g, h), wa_raw[g][:].rearrange("p t k -> p (t k)").bitcast(F32), 512 * h)
+
+        def empty_wa(g, h):
+            if g not in wa_grouped:
+                wa_grouped[g] = work.tile([P, 2048], BF16, name="wa_grouped", tag="wa_grouped", bufs=2, align_bytes=64)
+            empty_words(("k", g, h), wa_grouped[g][:, 1024 * h : 1024 * (h + 1)])
 
         def quant_wa(g):
             quantize("W" + str(g), wa_grouped[g][:], 512)
 
         wb_grouped = keep.tile([P, 4096], BF16, name="wb_grouped", align_bytes=64)
 
-        def prep_wb(h):
-            words = wb_raw[:].rearrange("p i m -> p (i m)").bitcast(F32)
-            bank = s_bank(F32, [P, 2, 2, P], "wb_t")
-            for s in range(2):
-                for u in range(2):
-                    w0 = 256 * (2 * h + s) + u
-                    nc.tensor.transpose(bank[:, s, u, :], words[:, w0 : w0 + 255 : 2], id_f32[:])
-            dst = wb_grouped[:, 1024 * h : 1024 * (h + 1)].bitcast(F32).rearrange("p (s j u) -> p s j u", s=2, u=2)
-            nc.scalar.copy(out=dst, in_=bank[:].rearrange("p s u j -> p s j u"))
+        def fill_wb(h):
+            fill_words(("b", h), wb_raw[0][:].rearrange("p i m -> p (i m)").bitcast(F32), 512 * h)
+
+        def empty_wb(h):
+            empty_words(("b", h), wb_grouped[:, 1024 * h : 1024 * (h + 1)])
 
         ft_t = keep.tile([P, 4, P], F32, name="ft_t")
 
-        def prep_ft():
-            bank = s_bank(F32, [P, 4, P], "ft_tp")
+        def fill_ft():
+            bank = side_bank["f"] = s_bank(F32, [P, 4, P], "ft_tp")
             for w in range(4):
                 nc.tensor.transpose(bank[:, w, :], ft_raw[:].bitcast(F32)[:, 128 * w : 128 * (w + 1)], id_f32[:])
-            nc.scalar.copy(out=ft_t[:], in_=bank[:])
+
+        def empty_ft():
+            nc.scalar.copy(out=ft_t[:], in_=side_bank["f"][:])
 
         w2_t = {}
 
-        def prep_w2(h, w):
-            if w == 0:
-                w2_t[h] = work.tile([P, 4, 512], F32, name="w2_t", tag="w2_t", bufs=1)
+        def fill_w2(h, w):
             words = w2_raw[h][:].rearrange("p i k -> p (i k)").bitcast(F32)
-            bank = s_bank(F32, [P, 4, P], "w2_tp")
+            bank = side_bank["2", h, w] = s_bank(F32, [P, 4, P], "w2_tp")
             for i in range(4):
                 nc.tensor.transpose(bank[:, i, :], words[:, 512 * i + 128 * w : 512 * i + 128 * (w + 1)], id_f32[:])
-            nc.scalar.copy(out=w2_t[h][:, w, :], in_=bank[:].rearrange("p i o -> p (i o)"))
+
+        def empty_w2(h, w):
+            if h not in w2_t:
+                w2_t[h] = work.tile([P, 4, 512], F32, name="w2_t", tag="w2_t", bufs=1)
+            nc.scalar.copy(out=w2_t[h][:, w, :], in_=side_bank["2", h, w][:].rearrange("p i o -> p (i o)"))
 
         ft2 = keep.tile([P, C], F32, name="ft2")
 
-        def fc2(h):
-            bank = s_bank(F32, [P, 512], "fc2_acc")
-            for w in range(4):
-                for e in range(2):
-                    nc.tensor.matmul(
-                        bank[:],
-                        lhsT=ft_t[:, w, :].bitcast(BF16)[:, e : e + 255 : 2],
-                        rhs=w2_t[h][:, w, :].bitcast(BF16)[:, e : e + 1023 : 2],
-                        start=(w == 0 and e == 0),
-                        stop=(w == 3 and e == 1),
-                    )
-            cols = slice(512 * h, 512 * (h + 1))
-            nc.vector.tensor_tensor(out=ft2[:, cols], in0=bank[:], in1=bf_t[:, cols], op=ALU.add)
+        fc2_bank = {}
+
+        def fc2_unit(h, n):
+            if n == 0:
+                fc2_bank[h] = s_bank(F32, [P, 512], "fc2_acc")
+            w, e = divmod(n, 2)
+            nc.tensor.matmul(
+                fc2_bank[h][:],
+                lhsT=ft_t[:, w, :].bitcast(BF16)[:, e : e + 255 : 2],
+                rhs=w2_t[h][:, w, :].bitcast(BF16)[:, e : e + 1023 : 2],
+                start=(n == 0),
+                stop=(n == 7),
+            )
+
+        def fc2_bias(h):
+            if True:
+                cols = slice(512 * h, 512 * (h + 1))
+                nc.vector.tensor_tensor(out=ft2[:, cols], in0=fc2_bank[h][:], in1=bf_t[:, cols], op=ALU.add)
 
         acc = {}
 
-        def conv1(kind, g):
+        def conv1_unit(kind, g, t):
+            if g == 0:
+                acc[t] = psum.tile([P, 512], F32, name="acc", tag="acc%d" % t)
+            w, cols = "W" + str(g), slice(P * t, P * (t + 1))
+            nc.tensor.matmul_mx(
+                out=acc[t][:],
+                lhsT=codes[w][:, cols].bitcast(FP8X4),
+                lhsT_scale=planes[w][:, cols],
+                rhs=codes[kind + str(g)][:].bitcast(FP8X4),
+                rhs_scale=planes[kind + str(g)][:],
+                start=(g == 0),
+                stop=(g == G - 1),
+            )
+
+        def conv1_last_pixel(g):
             for t in range(4):
                 if g == 0:
-                    acc[t] = psum.tile([P, 512], F32, name="acc", tag="acc%d" % t)
+                    acc[t] = psum.tile([P, P], F32, name="acc_c", tag="acc%d" % t)
+                w, cols, c = "W" + str(g), slice(P * t, P * (t + 1)), "C" + str(g - g % 2)
+                x = slice(P * (g % 2), P * (g % 2 + 1))
                 nc.tensor.matmul_mx(
                     out=acc[t][:],
-                    lhsT=codes["W" + str(g)][:, P * t : P * (t + 1)].bitcast(FP8X4),
-                    lhsT_scale=planes["W" + str(g)][:, P * t : P * (t + 1)],
-                    rhs=codes[kind + str(g)][:].bitcast(FP8X4),
-                    rhs_scale=planes[kind + str(g)][:],
+                    lhsT=codes[w][:, cols].bitcast(FP8X4),
+                    lhsT_scale=planes[w][:, cols],
+                    rhs=codes[c][:, x].bitcast(FP8X4),
+                    rhs_scale=planes[c][:, x],
                     start=(g == 0),
                     stop=(g == G - 1),
                 )
 
         hid = {}
 
-        def relu(kind):
-            t4 = work.tile([P, 4, 512], BF16, name="hid", tag="hid", bufs=1)
-            for t in range(4):
-                nc.scalar.activation(out=t4[:, t, :], in_=acc[t][:], func=ACT.Relu, bias=ba_t[:, t : t + 1])
-            hid[kind] = t4
+        def relu(kind, n, t):
+            if kind not in hid:
+                hid[kind] = work.tile([P, 4, n], BF16, name="hid", tag="hid_%d" % n, bufs=1)
+            nc.scalar.activation(
+                out=hid[kind][:, t, :], in_=acc[t][:], func=ACT.Relu, bias=ba_t[:, t : t + 1]
+            )
 
         def interleave(kind, n):
             t = work.tile([P, n, 4], BF16, name="hid_grouped" + kind, tag="hid_grouped_%d" % n, bufs=1, align_bytes=64)
@@ -251,117 +319,109 @@ def tile_joint_module_pb_kernel(tc, fv_bytes, fv_scale, ft, Wa, ba, Wb, bb, Wfc2
 
         s2 = {}
 
-        def conv2(kind, npix, first, last):
-            for x in range(npix):
-                for h in range(2):
-                    nc.tensor.matmul_mx(
-                        out=s2[h][:],
-                        lhsT=codes["H" + kind][:, P * x : P * (x + 1)].bitcast(FP8X4),
-                        lhsT_scale=planes["H" + kind][:, P * x : P * (x + 1)],
-                        rhs=codes["WB"][:, 512 * h : 512 * (h + 1)].bitcast(FP8X4),
-                        rhs_scale=planes["WB"][:, 512 * h : 512 * (h + 1)],
-                        start=(first and x == 0),
-                        stop=(last and x == npix - 1),
-                    )
+        def conv2_unit(kind, x, h):
+            if kind == "A" and x == 0:
+                s2[h] = psum.tile([P, 512], F32, name="s2", tag=("x3", "x%d" % (turn["n"] % 3))[h])
+            nc.tensor.matmul_mx(
+                out=s2[h][:],
+                lhsT=codes["H" + kind][:, P * x : P * (x + 1)].bitcast(FP8X4),
+                lhsT_scale=planes["H" + kind][:, P * x : P * (x + 1)],
+                rhs=codes["WB"][:, 512 * h : 512 * (h + 1)].bitcast(FP8X4),
+                rhs_scale=planes["WB"][:, 512 * h : 512 * (h + 1)],
+                start=(kind == "A" and x == 0),
+                stop=(kind == "C"),
+            )
 
-        A, Bq = [0, 1, 2, 3], [4, 5, 6, 7]
-        plans = {0: "SVVV", 1: "SSVV", 2: "SSSV", 3: "SSSS", 4: "SSSS", 5: "SSSS"}
-        widen(0, plans[0])
-        for s in range(8):
-            if s == 0:
-                load_fv(3)
-                load_wa(3)
+        loads = LOADS.split()
+        room = {"f": 7, "k": 3, "2": 2, "b": 2, "t": 1, "i": 2}
+        used = {}
+
+        def load(n):
+            if n[0] == "f":
+                g, h = int(n[1]), int(n[3])
+                fvb[g, h] = raw.tile([P, 2304], U8, name="fvb", tag="fvb", bufs=7)
+                c0 = g * 4608 + h * 2304
+                nc.sync.dma_start(out=fvb[g, h][:], in_=fv_rows[:, c0 : c0 + 2304])
+            elif n[0] == "k":
+                load_wa(int(n[1]))
+            elif n[0] == "2":
+                load_w2(int(n[1]))
+            elif n[0] == "t":
                 nc.sync.dma_start(out=ft_raw[:], in_=ft)
-                load_w2(0)
-            if s == 1:
-                load_fv(4)
-                load_wa(4)
-                nc.sync.dma_start(out=wb_raw[:], in_=wb_rows)
-            if s == 2:
-                load_fv(5)
-                load_wa(5)
-                load_w2(1)
+            elif n[0] == "b":
+                wb_raw[0] = raw.tile([P, 8, HID], BF16, name="wb_raw", tag="big8", bufs=2)
+                nc.sync.dma_start(out=wb_raw[0][:], in_=wb_rows)
+            elif n == "i":
                 nc.sync.dma_start(out=bf_t[:], in_=bfc2.partition_broadcast(P))
+            else:
                 nc.sync.dma_start(out=bb_t[:], in_=bb.partition_broadcast(P))
-            if s + 1 < G:
-                widen(s + 1, plans[s + 1])
-            if s < G:
-                prep_fv("A", s, A)
-                prep_wa(s)
-            if 1 <= s <= G:
-                conv1("A", s - 1)
-            if s == G:
-                relu("A")
-            if 2 <= s:
-                prep_fv("B", s - 2, Bq)
-                if s % 2 == 1:
-                    prep_c(s - 3)
-            if s == 2:
-                prep_ft()
-                prep_w2(0, 0)
-                prep_w2(0, 1)
-            if s == 3:
-                prep_w2(0, 2)
-                prep_w2(0, 3)
-                prep_wb(0)
-                prep_wb(1)
-            if s == 4:
-                fc2(0)
-                prep_wb(2)
-                prep_wb(3)
-            if s == 5:
-                prep_w2(1, 0)
-                prep_w2(1, 1)
-            if s == 6:
-                prep_w2(1, 2)
-                prep_w2(1, 3)
-                fc2(1)
-            if s < G:
-                quant_fv("A", s)
-                quant_wa(s)
-            if 2 <= s:
-                quant_fv("B", s - 2)
-                if s % 2 == 1:
-                    quant_c(s - 3)
-            if s == 5:
-                quantize("WB", wb_grouped[:], 1024)
-            if s == 6:
-                interleave("A", 512)
-                quant_h("A", 512)
-                conv1("B", 0)
-                conv1("B", 1)
-                conv1("B", 2)
-            if s == 7:
-                conv1("B", 3)
-                turn["banks"] = 2
-                s2[0] = psum.tile([P, 512], F32, name="s2_0", tag="x3")
-                s2[1] = psum.tile([P, 512], F32, name="s2_1", tag="x2")
-                conv2("A", 4, True, False)
-        conv1("B", 4)
-        conv1("B", 5)
-        relu("B")
-        cbank = x_bank(F32, [P, 4, P], "acc_c")
-        for t in range(4):
-            for g in range(G):
-                key = "C" + str(g - g % 2)
-                nc.tensor.matmul_mx(
-                    out=cbank[:, t, :],
-                    lhsT=codes["W" + str(g)][:, P * t : P * (t + 1)].bitcast(FP8X4),
-                    lhsT_scale=planes["W" + str(g)][:, P * t : P * (t + 1)],
-                    rhs=codes[key][:, P * (g % 2) : P * (g % 2 + 1)].bitcast(FP8X4),
-                    rhs_scale=planes[key][:, P * (g % 2) : P * (g % 2 + 1)],
-                    start=(g == 0),
-                    stop=(g == G - 1),
-                )
-        hid["C"] = work.tile([P, 4, P], BF16, name="hid_c", tag="hid_c", bufs=1)
-        for t in range(4):
-            nc.scalar.activation(out=hid["C"][:, t, :], in_=cbank[:, t, :], func=ACT.Relu, bias=ba_t[:, t : t + 1])
-        interleave("B", 512)
-        interleave("C", P)
-        quant_h("B", 512)
-        quant_h("C", P)
-        conv2("B", 4, False, False)
-        conv2("C", 1, False, True)
+
+        def pump():
+            while loads and room[loads[0][0]] > 0:
+                n = loads.pop(0)
+                load(n)
+                for k in "2b" if n[0] in "2b" else n[0]:
+                    room[k] -= 1
+
+        def used_up(key, kinds, count):
+            used[key] = used.get(key, 0) + 1
+            if used[key] == count:
+                for k in kinds:
+                    room[k] += 1
+                pump()
+
+        pump()
+
+        for step in " ".join(STEPS).split():
+            a = step[1:].split(".")
+            k = step[0]
+            if k == "w" or k == "v":
+                widen(int(a[0]), int(a[1]), k == "v")
+                used_up(("f", a[0], int(a[1]) // 2), "f", 2)
+            elif k == "T" or k == "E":
+                s = a[0][0]
+                if s == "k":
+                    (fill_wa if k == "T" else empty_wa)(int(a[0][1]), int(a[1]))
+                elif s == "2":
+                    (fill_w2 if k == "T" else empty_w2)(int(a[0][1]), int(a[1]))
+                elif s == "b":
+                    (fill_wb if k == "T" else empty_wb)(int(a[0][1]))
+                elif s == "f":
+                    (fill_ft if k == "T" else empty_ft)()
+                elif s == "F":
+                    fc2_bias(int(a[0][1]))
+                else:
+                    (fill if k == "T" else empty)(s, int(a[0][1]), int(a[1]))
+                if k == "T" and s == "k":
+                    used_up(a[0], "k", 2)
+                elif k == "T" and s == "2":
+                    used_up(a[0], "2b", 4)
+                elif k == "T" and s == "b":
+                    used_up("b", "2b", 4)
+            elif k == "q":
+                if a[0] == "b":
+                    quantize("WB", wb_grouped[:], 1024)
+                elif a[0][0] == "h":
+                    quant_h(a[0][1], P if a[0][1] == "C" else 512)
+                elif a[0][0] == "W":
+                    quant_wa(int(a[0][1]))
+                elif a[0][0] == "C":
+                    quant_c(int(a[0][1]))
+                else:
+                    quant_fv(a[0][0], int(a[0][1]))
+            elif k == "m":
+                if a[0] == "F":
+                    fc2_unit(int(a[1]), int(a[2]))
+                elif a[0] == "s":
+                    conv2_unit(a[1], int(a[2]), int(a[3]))
+                elif a[1] == "C":
+                    conv1_last_pixel(int(a[2]))
+                else:
+                    conv1_unit(a[1], int(a[2]), int(a[3]))
+            elif k == "R":
+                relu(a[0][0], P if a[0][0] == "C" else 512, int(a[0][1]))
+            elif k == "I":
+                interleave(a[0], P if a[0] == "C" else 512)
 
         z = keep.tile([P, C], F32, name="z")
         gate = keep.tile([P, C], F32, name="gate")

from contextlib import ExitStack

import concourse.mybir as mybir
from concourse.masks import make_identity

F32 = mybir.dt.float32
BF16 = mybir.dt.bfloat16
U32 = mybir.dt.uint32
U8 = mybir.dt.uint8
FP8 = mybir.dt.float8_e4m3fn
FP8X4 = mybir.dt.float8_e4m3fn_x4
ALU = mybir.AluOpType
ACT = mybir.ActivationFunctionType

B, C3, HID, C = 128, 3072, 512, 1024
PIX = 9
P = 128
G = C3 // 512

WARM = 56

FLOPS = 2 * (C3 * HID + HID * C) * B * PIX + 2 * B * C * C


LOADS = "f0.0 f0.1 k0 f1.0 f1.1 k1 f2.0 f2.1 20 f3.0 f3.1 k2 21 f4.0 f4.1 k3 f5.0 i f5.1 t i2 k4 k5 b"
STEPS = [
    "v0.0 w0.1 v0.2 w0.3 Tk0.0 v1.0 w1.1 TA0.0 v1.2 TA0.1 Ek0.0 EA0.0",
    "w1.3 Tk0.1 v2.0 Ek0.1 v2.1 TA1.0 w2.2 Tk1.0 qW0 TA1.1 EA0.1",
    "Ek1.0 EA1.0",
    "w2.3 T20.0 qA0 E20.0 TA2.0 EA1.1",
    "w3.0 Tk1.1 mm.A.0.0 EA2.0",
    "mm.A.0.1 Ek1.1 mm.A.0.2 w3.1 mm.A.0.3 qA1 T20.1 qW1 TA2.1 E20.1 TB0.0 EA2.1",
    "w3.2 T20.2 mm.A.1.0 mm.A.1.1 EB0.0",
    "mm.A.1.2 E20.2 mm.A.1.3 TB0.1 w3.3 qA2 Tk2.0 EB0.1",
    "TB1.0 Ek2.0 TB1.1 w4.0 EB1.0",
    "T20.3 TA3.0 qB0 E20.3 TA3.1 v4.1 w4.2 EB1.1",
    "Tf w4.3 v5.0 qB1 Ef TA4.0 EA3.0",
    "w5.1 mF.0.0 EA3.1",
    "mF.0.1 w5.2 mF.0.2 EA4.0",
    "mF.0.3 mF.0.4 w5.3 mF.0.5 mF.0.6 qA3 mF.0.7 TA4.1 EF0 TA5.0 EA4.1",
    "Tk2.1 TA5.1 Ek2.1 EA5.0",
    "TB2.0 Tk3.0 qA4 TB2.1 Ek3.0 qW2 EA5.1",
    "Tk3.1 mm.A.2.0 Ek3.1 EB2.0",
    "mm.A.2.1 mm.A.2.2 qA5 mm.A.2.3 qW3 Tk4.0 EB2.1",
    "TB3.0 Ek4.0 mm.A.3.0 mm.A.3.1 EB3.0",
    "mm.A.3.2 mm.A.3.3 Tk4.1 qB2 TB3.1 Ek4.1 TB4.0 EB3.1",
    "Tk5.0 TB4.1 Ek5.0 qW4 TC0.0 qB3 Tk5.1 EB4.0",
    "mm.A.4.0 Ek5.1 mm.A.4.1 qW5 mm.A.4.2 EB4.1",
    "mm.A.4.3 mm.A.5.0 mm.A.5.1 RA0 EC0.0",
    "Tb3 RA1 mm.A.5.2 mm.A.5.3 Eb3 qB4 mm.B.0.0 mm.B.0.1 RA2 qC0 T21.0 TB5.0 RA3 E21.0 mm.B.0.2 IA mm.B.0.3 mm.B.1.0 T21.1 mm.B.1.1 EB5.0",
    "E21.1 mm.B.1.2 mm.B.1.3 Tb2 qhA mm.B.2.0 Eb2 mm.B.2.1 mm.B.2.2 Tb0 mm.B.2.3 Eb0 mm.B.3.0 mm.B.3.1 Tb1 mm.B.3.2 Eb1 mm.B.3.3 mm.B.4.0 qb T21.2 mm.B.4.1 E21.2 mm.B.4.2 mm.B.4.3 T21.3 TB5.1 E21.3 TC2.0 EB5.1",
    "mF.1.0 mF.1.1 mF.1.2 EC2.0",
    "mF.1.3 mF.1.4 mF.1.5 mF.1.6 mF.1.7 qB5 TC4.0 qC2 mm.B.5.0 EF1 mm.B.5.1 RB0 mm.B.5.2 EC4.0",
    "mm.B.5.3 RB1 ms.A.0.0 ms.A.0.1 ms.A.1.0 RB2 ms.A.1.1 qC4 ms.A.2.0 RB3 mm.C.0.4 IB mm.C.1.4 mm.C.2.4 mm.C.3.4 mm.C.4.4 mm.C.5.4 qhB ms.A.2.1 RC0 ms.A.3.0 RC1 ms.A.3.1 RC2 ms.B.0.0 RC3 ms.B.0.1 IC ms.B.1.0 ms.B.1.1 qhC ms.B.2.0 ms.B.2.1 ms.B.3.0 ms.B.3.1 ms.C.0.0 ms.C.0.1",
]


def tile_joint_module_pb_kernel(tc, fv_bytes, fv_scale, ft, Wa, ba, Wb, bb, Wfc2, bfc2, out):
    nc = tc.nc
    with ExitStack() as ctx:
        keep = ctx.enter_context(tc.tile_pool(name="keep", bufs=1))
        raw = ctx.enter_context(tc.tile_pool(name="raw", bufs=4))
        work = ctx.enter_context(tc.tile_pool(name="work", bufs=2))
        psum = ctx.enter_context(tc.psum_pool(name="psum", bufs=1))

        id_f32 = keep.tile([P, P], F32, name="id_f32")
        id_bf = keep.tile([P, P], BF16, name="id_bf")
        make_identity(nc, id_bf[:])
        make_identity(nc, id_f32[:])

        sc = keep.tile([P, G, 4], F32, name="sc")
        ba_t = keep.tile([P, 4], BF16, name="ba_t")
        bb_t = keep.tile([P, C], BF16, name="bb_t")
        bf_t = keep.tile([P, C], BF16, name="bf_t")
        dummy = keep.tile([P, 1], F32, name="dummy")

        ctx.enter_context(tc.manual_schedule())

        fv_rows = fv_bytes.rearrange("b c i j -> b (c i j)")
        wa_rows = Wa.rearrange("(m t) k -> m t k", t=4)
        wb_rows = Wb.rearrange("(i p) m -> p i m", p=P)
        w2_rows = Wfc2.rearrange("(i p) k -> p i k", p=P)

        fvb = {}

        wa_raw = {}

        def load_wa(g):
            t = raw.tile([P, 4, 512], BF16, name="wa_raw", tag="wa_raw", bufs=3)
            nc.sync.dma_start(out=t[:], in_=wa_rows[:, :, 512 * g : 512 * (g + 1)])
            wa_raw[g] = t

        w2_raw = {}

        def load_w2(h):
            t = raw.tile([P, 4, 1024], BF16, name="w2_raw", tag="big8", bufs=2)
            nc.sync.dma_start(out=t[:], in_=w2_rows[:, 4 * h : 4 * h + 4, :])
            w2_raw[h] = t

        ft_raw = keep.tile([P, C], BF16, name="ft_raw")
        wb_raw = {}

        nc.scalar.dma_start(out=sc[:], in_=fv_scale.rearrange("o (g p t) i j -> p (o g) (t i j)", p=P, t=4))
        nc.scalar.dma_start(out=ba_t[:], in_=ba.rearrange("(p t) -> p t", t=4))
        nc.vector.memset(dummy[:], 0.0)
        nc.scalar.activation(out=dummy[:], in_=dummy[:], func=ACT.Sigmoid)

        wide = {}

        def widen(g, q, on_vector):
            if g not in wide:
                wide[g] = work.tile([P, 4608], BF16, name="wide", tag="wide", bufs=6)
            src = fvb[g, q // 2][:, (q % 2) * 1152 : (q % 2 + 1) * 1152].bitcast(FP8)
            dst = wide[g][:, q * 1152 : (q + 1) * 1152]
            if on_vector:
                nc.vector.tensor_copy(out=dst, in_=src)
            else:
                nc.scalar.copy(out=dst, in_=src)

        turn = {"n": 0, "banks": 3}

        def x_bank(dtype, shape, name):
            k = turn["n"] % turn["banks"]
            turn["n"] += 1
            return psum.tile(shape, dtype, name=name, tag="x%d" % k)

        def s_bank(dtype, shape, name):
            return psum.tile(shape, dtype, name=name, tag="x3")

        by_matmul = {"left": WARM}

        def transposes_fv(bank, slot, g, pix):
            for t in range(4):
                e = 9 * t + pix
                src = wide[g][:, e : e + 36 * 127 + 1 : 36]
                if by_matmul["left"] > 0:
                    by_matmul["left"] -= 1
                    nc.tensor.matmul(bank[:, slot, t, :], lhsT=src, rhs=id_bf[:], start=True, stop=True)
                else:
                    nc.tensor.transpose(bank[:, slot, t, :], src, id_bf[:])

        def scaled(dst, bank, slots, scale):
            nc.vector.tensor_tensor(
                out=dst, in0=bank[:, slots, :, :].rearrange("p x t b -> p x b t"), in1=scale, op=ALU.mult
            )

        codes, planes = {}, {}

        def quantize(key, src, n):
            codes[key] = keep.tile([P, n], U32, name="codes_" + key, align_bytes=64)
            planes[key] = keep.tile([P, n], U8, name="planes_" + key, align_bytes=64)
            nc.vector.quantize_mx(out=codes[key][:].bitcast(FP8X4), scales=planes[key][:], in_=src)

        grouped = {}

        def fill(kind, g, h):
            bank = x_bank(BF16, [P, 2, 4, P], "fv_t")
            for s in range(2):
                if kind == "C":
                    transposes_fv(bank, s, g + s, 8)
                else:
                    transposes_fv(bank, s, g, (0 if kind == "A" else 4) + 2 * h + s)
            fbank[kind, g, h] = bank

        fbank = {}

        def empty(kind, g, h):
            bank = fbank[kind, g, h]
            if kind == "C":
                t = work.tile([P, 2, P, 4], BF16, name="c_grouped", tag="c_grouped", bufs=2, align_bytes=64)
                scaled(t[:], bank, slice(0, 2), sc[:, g : g + 2, :].unsqueeze(2).to_broadcast([P, 2, P, 4]))
                grouped["C" + str(g)] = t
                return
            if h == 0:
                grouped[kind + str(g)] = work.tile(
                    [P, 4, P, 4], BF16, name="fv_grouped", tag="fv_grouped", bufs=3, align_bytes=64
                )
            t = grouped[kind + str(g)]
            scale = sc[:, g, :].unsqueeze(1).unsqueeze(1).to_broadcast([P, 2, P, 4])
            scaled(t[:, 2 * h : 2 * h + 2, :, :], bank, slice(0, 2), scale)

        def quant_fv(kind, g):
            quantize(kind + str(g), grouped[kind + str(g)][:].rearrange("p x b t -> p (x b t)"), 512)

        def quant_c(g):
            quantize("C" + str(g), grouped["C" + str(g)][:].rearrange("p x b t -> p (x b t)"), 256)

        wa_grouped = {}

        side_bank = {}

        def fill_words(key, words, base):
            side_bank[key] = s_bank(F32, [P, 2, 2, P], "wt")
            for s in range(2):
                for u in range(2):
                    w0 = base + 256 * s + u
                    nc.tensor.transpose(side_bank[key][:, s, u, :], words[:, w0 : w0 + 255 : 2], id_f32[:])

        def empty_words(key, dst):
            nc.scalar.copy(
                out=dst.bitcast(F32).rearrange("p (s j u) -> p s j u", s=2, u=2),
                in_=side_bank[key][:].rearrange("p s u j -> p s j u"),
            )

        def fill_wa(g, h):
            fill_words(("k", g, h), wa_raw[g][:].rearrange("p t k -> p (t k)").bitcast(F32), 512 * h)

        def empty_wa(g, h):
            if g not in wa_grouped:
                wa_grouped[g] = work.tile([P, 2048], BF16, name="wa_grouped", tag="wa_grouped", bufs=2, align_bytes=64)
            empty_words(("k", g, h), wa_grouped[g][:, 1024 * h : 1024 * (h + 1)])

        def quant_wa(g):
            quantize("W" + str(g), wa_grouped[g][:], 512)

        wb_grouped = keep.tile([P, 4096], BF16, name="wb_grouped", align_bytes=64)

        def fill_wb(h):
            fill_words(("b", h), wb_raw[0][:].rearrange("p i m -> p (i m)").bitcast(F32), 512 * h)

        def empty_wb(h):
            empty_words(("b", h), wb_grouped[:, 1024 * h : 1024 * (h + 1)])

        ft_t = keep.tile([P, 4, P], F32, name="ft_t")

        def fill_ft():
            bank = side_bank["f"] = s_bank(F32, [P, 4, P], "ft_tp")
            for w in range(4):
                nc.tensor.transpose(bank[:, w, :], ft_raw[:].bitcast(F32)[:, 128 * w : 128 * (w + 1)], id_f32[:])

        def empty_ft():
            nc.scalar.copy(out=ft_t[:], in_=side_bank["f"][:])

        w2_t = {}

        def fill_w2(h, w):
            words = w2_raw[h][:].rearrange("p i k -> p (i k)").bitcast(F32)
            bank = side_bank["2", h, w] = s_bank(F32, [P, 4, P], "w2_tp")
            for i in range(4):
                nc.tensor.transpose(bank[:, i, :], words[:, 512 * i + 128 * w : 512 * i + 128 * (w + 1)], id_f32[:])

        def empty_w2(h, w):
            if h not in w2_t:
                w2_t[h] = work.tile([P, 4, 512], F32, name="w2_t", tag="w2_t", bufs=1)
            nc.scalar.copy(out=w2_t[h][:, w, :], in_=side_bank["2", h, w][:].rearrange("p i o -> p (i o)"))

        ft2 = keep.tile([P, C], F32, name="ft2")

        fc2_bank = {}

        def fc2_unit(h, n):
            if n == 0:
                fc2_bank[h] = s_bank(F32, [P, 512], "fc2_acc")
            w, e = divmod(n, 2)
            nc.tensor.matmul(
                fc2_bank[h][:],
                lhsT=ft_t[:, w, :].bitcast(BF16)[:, e : e + 255 : 2],
                rhs=w2_t[h][:, w, :].bitcast(BF16)[:, e : e + 1023 : 2],
                start=(n == 0),
                stop=(n == 7),
            )

        def fc2_bias(h):
            if True:
                cols = slice(512 * h, 512 * (h + 1))
                nc.vector.tensor_tensor(out=ft2[:, cols], in0=fc2_bank[h][:], in1=bf_t[:, cols], op=ALU.add)

        acc = {}

        def conv1_unit(kind, g, t):
            if g == 0:
                acc[t] = psum.tile([P, 512], F32, name="acc", tag="acc%d" % t)
            w, cols = "W" + str(g), slice(P * t, P * (t + 1))
            nc.tensor.matmul_mx(
                out=acc[t][:],
                lhsT=codes[w][:, cols].bitcast(FP8X4),
                lhsT_scale=planes[w][:, cols],
                rhs=codes[kind + str(g)][:].bitcast(FP8X4),
                rhs_scale=planes[kind + str(g)][:],
                start=(g == 0),
                stop=(g == G - 1),
            )

        def conv1_last_pixel(g):
            for t in range(4):
                if g == 0:
                    acc[t] = psum.tile([P, P], F32, name="acc_c", tag="acc%d" % t)
                w, cols, c = "W" + str(g), slice(P * t, P * (t + 1)), "C" + str(g - g % 2)
                x = slice(P * (g % 2), P * (g % 2 + 1))
                nc.tensor.matmul_mx(
                    out=acc[t][:],
                    lhsT=codes[w][:, cols].bitcast(FP8X4),
                    lhsT_scale=planes[w][:, cols],
                    rhs=codes[c][:, x].bitcast(FP8X4),
                    rhs_scale=planes[c][:, x],
                    start=(g == 0),
                    stop=(g == G - 1),
                )

        hid = {}

        def relu(kind, n, t):
            if kind not in hid:
                hid[kind] = work.tile([P, 4, n], BF16, name="hid", tag="hid_%d" % n, bufs=1)
            nc.scalar.activation(
                out=hid[kind][:, t, :], in_=acc[t][:], func=ACT.Relu, bias=ba_t[:, t : t + 1]
            )

        def interleave(kind, n):
            t = work.tile([P, n, 4], BF16, name="hid_grouped" + kind, tag="hid_grouped_%d" % n, bufs=1, align_bytes=64)
            nc.vector.tensor_copy(
                out=t[:].rearrange("p (c i) t -> p c t i", i=4),
                in_=hid[kind][:, :, 0:n].rearrange("p t (c i) -> p c t i", i=4),
            )
            grouped["H" + kind] = t

        def quant_h(kind, n):
            quantize("H" + kind, grouped["H" + kind][:].rearrange("p n t -> p (n t)"), n)

        s2 = {}

        def conv2_unit(kind, x, h):
            if kind == "A" and x == 0:
                s2[h] = psum.tile([P, 512], F32, name="s2", tag=("x3", "x%d" % (turn["n"] % 3))[h])
            nc.tensor.matmul_mx(
                out=s2[h][:],
                lhsT=codes["H" + kind][:, P * x : P * (x + 1)].bitcast(FP8X4),
                lhsT_scale=planes["H" + kind][:, P * x : P * (x + 1)],
                rhs=codes["WB"][:, 512 * h : 512 * (h + 1)].bitcast(FP8X4),
                rhs_scale=planes["WB"][:, 512 * h : 512 * (h + 1)],
                start=(kind == "A" and x == 0),
                stop=(kind == "C"),
            )

        loads = LOADS.split()
        room = {"f": 7, "k": 3, "2": 2, "b": 2, "t": 1, "i": 2}
        used = {}

        def load(n):
            if n[0] == "f":
                g, h = int(n[1]), int(n[3])
                fvb[g, h] = raw.tile([P, 2304], U8, name="fvb", tag="fvb", bufs=7)
                c0 = g * 4608 + h * 2304
                nc.sync.dma_start(out=fvb[g, h][:], in_=fv_rows[:, c0 : c0 + 2304])
            elif n[0] == "k":
                load_wa(int(n[1]))
            elif n[0] == "2":
                load_w2(int(n[1]))
            elif n[0] == "t":
                nc.sync.dma_start(out=ft_raw[:], in_=ft)
            elif n[0] == "b":
                wb_raw[0] = raw.tile([P, 8, HID], BF16, name="wb_raw", tag="big8", bufs=2)
                nc.sync.dma_start(out=wb_raw[0][:], in_=wb_rows)
            elif n == "i":
                nc.sync.dma_start(out=bf_t[:], in_=bfc2.partition_broadcast(P))
            else:
                nc.sync.dma_start(out=bb_t[:], in_=bb.partition_broadcast(P))

        def pump():
            while loads and room[loads[0][0]] > 0:
                n = loads.pop(0)
                load(n)
                for k in "2b" if n[0] in "2b" else n[0]:
                    room[k] -= 1

        def used_up(key, kinds, count):
            used[key] = used.get(key, 0) + 1
            if used[key] == count:
                for k in kinds:
                    room[k] += 1
                pump()

        pump()

        for step in " ".join(STEPS).split():
            a = step[1:].split(".")
            k = step[0]
            if k == "w" or k == "v":
                widen(int(a[0]), int(a[1]), k == "v")
                used_up(("f", a[0], int(a[1]) // 2), "f", 2)
            elif k == "T" or k == "E":
                s = a[0][0]
                if s == "k":
                    (fill_wa if k == "T" else empty_wa)(int(a[0][1]), int(a[1]))
                elif s == "2":
                    (fill_w2 if k == "T" else empty_w2)(int(a[0][1]), int(a[1]))
                elif s == "b":
                    (fill_wb if k == "T" else empty_wb)(int(a[0][1]))
                elif s == "f":
                    (fill_ft if k == "T" else empty_ft)()
                elif s == "F":
                    fc2_bias(int(a[0][1]))
                else:
                    (fill if k == "T" else empty)(s, int(a[0][1]), int(a[1]))
                if k == "T" and s == "k":
                    used_up(a[0], "k", 2)
                elif k == "T" and s == "2":
                    used_up(a[0], "2b", 4)
                elif k == "T" and s == "b":
                    used_up("b", "2b", 4)
            elif k == "q":
                if a[0] == "b":
                    quantize("WB", wb_grouped[:], 1024)
                elif a[0][0] == "h":
                    quant_h(a[0][1], P if a[0][1] == "C" else 512)
                elif a[0][0] == "W":
                    quant_wa(int(a[0][1]))
                elif a[0][0] == "C":
                    quant_c(int(a[0][1]))
                else:
                    quant_fv(a[0][0], int(a[0][1]))
            elif k == "m":
                if a[0] == "F":
                    fc2_unit(int(a[1]), int(a[2]))
                elif a[0] == "s":
                    conv2_unit(a[1], int(a[2]), int(a[3]))
                elif a[1] == "C":
                    conv1_last_pixel(int(a[2]))
                else:
                    conv1_unit(a[1], int(a[2]), int(a[3]))
            elif k == "R":
                relu(a[0][0], P if a[0][0] == "C" else 512, int(a[0][1]))
            elif k == "I":
                interleave(a[0], P if a[0] == "C" else 512)

        z = keep.tile([P, C], F32, name="z")
        gate = keep.tile([P, C], F32, name="gate")
        res = keep.tile([P, C], F32, name="res")
        for h in range(2):
            cols = slice(512 * h, 512 * (h + 1))
            nc.vector.scalar_tensor_tensor(
                out=z[:, cols], in0=s2[h][:], scalar=1.0 / PIX, in1=bb_t[:, cols], op0=ALU.mult, op1=ALU.add
            )
            nc.scalar.activation(out=gate[:, cols], in_=z[:, cols], func=ACT.Sigmoid)
            nc.vector.scalar_tensor_tensor(
                out=res[:, cols], in0=gate[:, cols], scalar=1.0, in1=ft2[:, cols], op0=ALU.add, op1=ALU.mult
            )
            nc.sync.dma_start(out=out[:, cols], in_=res[:, cols])
